import numpy as np
import ml_dtypes


def mxq(x, axis, fmt="e4m3"):
    dtype, down = {"e4m3": (ml_dtypes.float8_e4m3fn, 7), "e5m2": (ml_dtypes.float8_e5m2, 14)}[fmt]
    v = np.moveaxis(np.asarray(x, np.float32).astype(ml_dtypes.bfloat16).astype(np.float64), axis, -1)
    blocks = v.reshape(v.shape[:-1] + (-1, 32))
    amax = np.abs(blocks).max(-1, keepdims=True)
    byte = np.maximum(np.where(amax > 0, np.frexp(amax)[1] - 1 + 127, 0) - down, 1)
    scale = np.exp2(byte - 127.0)
    codes = (blocks / scale).astype(np.float32).astype(dtype).astype(np.float64)
    return np.moveaxis((codes * scale).reshape(v.shape), -1, axis)


WIDE = False


def mx_kscale(k):
    if not WIDE:
        return np.ones(k)
    levels = np.array([10, -10, 5, -5, 0])
    a = np.random.permutation(np.resize(levels, k // 512 * 4)).reshape(k // 512, 4)
    idx = np.arange(k)
    return np.exp2(a[idx // 512, idx % 128 // 32])


BF16 = ml_dtypes.bfloat16


def bf(x):
    return np.asarray(x, np.float32).astype(BF16)


def f64(x):
    return np.asarray(x).astype(np.float64)


B, N, E, L, A, H1, H2, G = 128, 8, 8, 6144, 2048, 128, 1024, 8
D = L + A
EPS = 1e-5


def mish(v):
    return v * np.tanh(np.log(1.0 + np.exp(v)))


def layer_norm(v, gamma, beta):
    mu = v.mean(-1, keepdims=True)
    var = v.var(-1, keepdims=True)
    return (v - mu) / np.sqrt(var + EPS) * gamma + beta


def setup_inputs():
    s = mx_kscale(D)
    r = np.random.standard_normal
    return {"tokens": bf(r((B, N, D)) * s),
            "logits": bf(r((B, N, E))),
            "W1": bf(r((E, D, H1)) / np.sqrt(D) / s[:, None]),
            "b1": bf(0.1 * r((E, H1))),
            "g1": bf(1.0 + 0.1 * r((E, H1))),
            "be1": bf(0.1 * r((E, H1)))}


def reference(tokens, logits, W1, b1, g1, be1):
    tok, lg = f64(tokens), f64(logits)
    ex = np.exp(lg - lg.max(1, keepdims=True))
    disp = ex / ex.sum(1, keepdims=True)
    slot = sum(disp[:, n, :].T[:, :, None] * tok[None, :, n, :] for n in range(N))
    h = (mxq(slot, 2, "e4m3") @ mxq(f64(W1), 1, "e4m3")) + f64(b1)[:, None, :]
    h = mish(layer_norm(h, f64(g1)[:, None, :], f64(be1)[:, None, :]))
    return h.transpose(1, 0, 2)

@@ -1,0 +1,225 @@
+from contextlib import ExitStack
+
+import concourse.mybir as mybir
+from concourse.masks import make_identity
+
+F32 = mybir.dt.float32
+BF16 = mybir.dt.bfloat16
+U32 = mybir.dt.uint32
+U8 = mybir.dt.uint8
+FP8X4 = mybir.dt.float8_e4m3fn_x4
+ALU = mybir.AluOpType
+ACT = mybir.ActivationFunctionType
+AXIS = mybir.AxisListType
+
+B, N, E, D, H1 = 128, 8, 8, 8192, 128
+EPS = 1e-5
+P = 128
+PACK = 4
+K_PASS = P * PACK
+PASSES = D // K_PASS
+CHUNK = 1024
+CHUNKS = D // CHUNK
+CHUNK_PASSES = CHUNK // K_PASS
+PAIRS = N // 2
+W_HALF_PASSES = PASSES // 2
+W_PIECE_PASSES = 4
+W_PIECES = PASSES // W_PIECE_PASSES
+W_PIECE_COLS = W_PIECE_PASSES * H1
+MISH_CLAMP = 20.0
+
+FLOPS = 2 * E * B * D * H1 + 2 * B * N * E * D
+
+
+def tile_softmoedynamics_pa_k_kernel(tc, tokens, logits, W1, b1, g1, be1, out):
+    nc = tc.nc
+    with ExitStack() as ctx:
+        const = ctx.enter_context(tc.tile_pool(name="const", bufs=1))
+        tok_pool = ctx.enter_context(tc.tile_pool(name="tok", bufs=1))
+        w_raw_pool = ctx.enter_context(tc.tile_pool(name="w_raw", bufs=2))
+        w_grp_pool = ctx.enter_context(tc.tile_pool(name="w_grp", bufs=2))
+        w_mx_pool = ctx.enter_context(tc.tile_pool(name="w_mx", bufs=2))
+        term_pool = ctx.enter_context(tc.tile_pool(name="term", bufs=6))
+        slot_pool = ctx.enter_context(tc.tile_pool(name="slot", bufs=2))
+        epi_pool = ctx.enter_context(tc.tile_pool(name="epi", bufs=2))
+        turned_pool = ctx.enter_context(tc.psum_pool(name="turned", bufs=6))
+        acc_pool = ctx.enter_context(tc.psum_pool(name="acc", bufs=2))
+
+        lg = const.tile([P, N, E], BF16)
+        nc.sync.dma_start(out=lg[:], in_=logits)
+
+        tok = []
+
+        def load_tokens(c):
+            tok_c = tok_pool.tile([P, N, CHUNK], BF16, name="tok%d" % c)
+            for q in range(PAIRS):
+                nc.sync.dma_start(
+                    out=tok_c[:, 2 * q : 2 * q + 2, :],
+                    in_=tokens[:, 2 * q : 2 * q + 2, c * CHUNK : (c + 1) * CHUNK],
+                )
+            tok.append(tok_c)
+
+        w_raw = {}
+
+        def load_w_half(e, half):
+            raw = w_raw_pool.tile([P, PACK, W_HALF_PASSES * H1], BF16, name="w_raw")
+            rows = W1[e, half * W_HALF_PASSES * K_PASS : (half + 1) * W_HALF_PASSES * K_PASS, :]
+            by_code = rows.rearrange("(g t p) h -> t p g h", t=PACK, p=P)
+            for t in range(PACK):
+                nc.sync.dma_start(
+                    out=raw[:, t, :].rearrange("p (g h) -> p g h", h=H1), in_=by_code[t]
+                )
+            w_raw[(e, half)] = raw
+
+        load_tokens(0)
+        load_w_half(0, 0)
+        load_tokens(1)
+        load_w_half(0, 1)
+        for c in range(2, CHUNKS):
+            load_tokens(c)
+
+        bias_bc = const.tile([P, E * H1], BF16)
+        gain_bc = const.tile([P, E * H1], BF16)
+        shift_bc = const.tile([P, E * H1], BF16)
+        for row_bc, vec in ((bias_bc, b1), (gain_bc, g1), (shift_bc, be1)):
+            nc.gpsimd.dma_start(
+                out=row_bc[:], in_=vec.rearrange("e h -> (e h)").partition_broadcast(P)
+            )
+
+        ident = const.tile([P, P], F32)
+        make_identity(nc, ident[:])
+        minus_half = const.tile([P, 1], F32)
+        nc.vector.memset(minus_half[:], -0.5)
+
+        lg_en = lg[:].rearrange("p n e -> p e n")
+        top = const.tile([P, E], F32)
+        nc.vector.tensor_reduce(out=top[:], in_=lg_en, axis=AXIS.X, op=ALU.max)
+        disp = const.tile([P, E, N], F32)
+        nc.vector.tensor_tensor(
+            out=disp[:], in0=lg_en, in1=top[:].unsqueeze(2).to_broadcast([P, E, N]), op=ALU.subtract
+        )
+        nc.scalar.activation(out=disp[:], in_=disp[:], func=ACT.Exp)
+        total = const.tile([P, E], F32)
+        nc.vector.tensor_reduce(out=total[:], in_=disp[:], axis=AXIS.X, op=ALU.add)
+        nc.vector.reciprocal(out=total[:], in_=total[:])
+        nc.vector.tensor_tensor(
+            out=disp[:], in0=disp[:], in1=total[:].unsqueeze(2).to_broadcast([P, E, N]), op=ALU.mult
+        )
+
+        w_codes = {}
+        w_scales = {}
+
+        def new_w_mx(e):
+            w_codes[e] = w_mx_pool.tile([P, PASSES * H1], U32, name="w_codes", align_bytes=64)
+            w_scales[e] = w_mx_pool.tile([P, PASSES * H1], U8, name="w_scales", align_bytes=64)
+
+        def quantise_w_piece(e, piece):
+            pieces_per_half = W_PIECES // 2
+            raw = w_raw[(e, piece // pieces_per_half)]
+            first = (piece % pieces_per_half) * W_PIECE_COLS
+            grouped = w_grp_pool.tile([P, W_PIECE_COLS, PACK], BF16, name="w_grp", align_bytes=64)
+            nc.vector.tensor_copy(
+                out=grouped[:].rearrange("p (c i) t -> p c t i", i=4),
+                in_=raw[:, :, first : first + W_PIECE_COLS].rearrange("p t (c i) -> p c t i", i=4),
+            )
+            cols = slice(piece * W_PIECE_COLS, (piece + 1) * W_PIECE_COLS)
+            nc.vector.quantize_mx(
+                out=w_codes[e][:, cols].bitcast(FP8X4),
+                scales=w_scales[e][:, cols],
+                in_=grouped[:].rearrange("p w t -> p (w t)"),
+            )
+
+        new_w_mx(0)
+        for piece in range(W_PIECES):
+            quantise_w_piece(0, piece)
+        load_w_half(1, 0)
+        load_w_half(1, 1)
+
+        def finish_expert(e, acc):
+            cols = slice(e * H1, (e + 1) * H1)
+            v = epi_pool.tile([P, H1], F32, name="v")
+            nc.vector.tensor_tensor(out=v[:], in0=acc[:], in1=bias_bc[:, cols], op=ALU.add)
+            stats = epi_pool.tile([P, 6], F32, name="stats")
+            nc.vector.bn_stats(out=stats[:], in_=v[:])
+            mean_var = epi_pool.tile([P, 2], F32, name="mean_var")
+            nc.vector.bn_aggr(out=mean_var[:], in_=stats[:])
+            rstd = epi_pool.tile([P, 1], F32, name="rstd")
+            nc.gpsimd.tensor_scalar(
+                out=rstd[:], in0=mean_var[:, 1:2], scalar1=EPS, scalar2=1.0, op0=ALU.add, op1=ALU.mult
+            )
+            nc.gpsimd.tensor_tensor(out=rstd[:], in0=rstd[:], in1=minus_half[:], op=ALU.pow)
+            nc.vector.tensor_scalar(
+                out=v[:], in0=v[:], scalar1=mean_var[:, 0:1], scalar2=rstd[:],
+                op0=ALU.subtract, op1=ALU.mult,
+            )
+            nc.vector.tensor_tensor(out=v[:], in0=v[:], in1=gain_bc[:, cols], op=ALU.mult)
+            nc.vector.tensor_tensor(out=v[:], in0=v[:], in1=shift_bc[:, cols], op=ALU.add)
+            w = epi_pool.tile([P, H1], F32, name="w")
+            nc.vector.tensor_scalar_min(out=w[:], in0=v[:], scalar1=MISH_CLAMP)
+            nc.scalar.activation(out=w[:], in_=w[:], func=ACT.Exp)
+            n = epi_pool.tile([P, H1], F32, name="n")
+            nc.vector.scalar_tensor_tensor(
+                out=n[:], in0=w[:], scalar=2.0, in1=w[:], op0=ALU.add, op1=ALU.mult
+            )
+            nc.vector.tensor_scalar_add(out=w[:], in0=n[:], scalar1=2.0)
+            nc.vector.reciprocal(out=w[:], in_=w[:])
+            nc.vector.tensor_tensor(out=n[:], in0=n[:], in1=v[:], op=ALU.mult)
+            nc.vector.tensor_tensor(out=n[:], in0=n[:], in1=w[:], op=ALU.mult)
+            nc.sync.dma_start(out=out[:, e, :], in_=n[:])
+
+        for e in range(E):
+            acc = acc_pool.tile([P, H1], F32, name="acc")
+            if e + 1 < E:
+                new_w_mx(e + 1)
+            for c in range(CHUNKS):
+                if e + 1 < E and c % 2 == 0:
+                    piece = c // 2
+                    quantise_w_piece(e + 1, piece)
+                    if e + 2 < E and piece % 2 == 1:
+                        load_w_half(e + 2, piece // 2)
+
+                turned = [
+                    turned_pool.tile([P, PACK, B], F32, name="turned") for g in range(CHUNK_PASSES)
+                ]
+                for q in range(PAIRS):
+                    term = term_pool.tile([P, CHUNK], F32, name="term")
+                    nc.scalar.activation(
+                        out=term[:], in_=tok[c][:, 2 * q, :], func=ACT.Copy,
+                        scale=disp[:, e, 2 * q : 2 * q + 1],
+                    )
+                    nc.vector.scalar_tensor_tensor(
+                        out=term[:], in0=tok[c][:, 2 * q + 1, :],
+                        scalar=disp[:, e, 2 * q + 1 : 2 * q + 2], in1=term[:],
+                        op0=ALU.mult, op1=ALU.add,
+                    )
+                    for g in range(CHUNK_PASSES):
+                        for t in range(PACK):
+                            first = (g * PACK + t) * P
+                            nc.tensor.matmul(
+                                out=turned[g][:, t, :], lhsT=term[:, first : first + P], rhs=ident[:],
+                                is_transpose=True,
+                                start=(q == 0 and t == 0), stop=(q == PAIRS - 1 and t == PACK - 1),
+                            )
+
+                grouped = slot_pool.tile([P, CHUNK_PASSES, B, PACK], BF16, name="grouped", align_bytes=64)
+                for g in range(CHUNK_PASSES):
+                    nc.scalar.copy(out=grouped[:, g, :, :], in_=turned[g][:].rearrange("p t b -> p b t"))
+                s_codes = slot_pool.tile([P, CHUNK_PASSES * B], U32, name="s_codes", align_bytes=64)
+                s_scales = slot_pool.tile([P, CHUNK_PASSES * B], U8, name="s_scales", align_bytes=64)
+                nc.vector.quantize_mx(
+                    out=s_codes[:].bitcast(FP8X4),
+                    scales=s_scales[:],
+                    in_=grouped[:].rearrange("p g b t -> p (g b t)"),
+                )
+                for g in range(CHUNK_PASSES):
+                    k = c * CHUNK_PASSES + g
+                    nc.tensor.matmul_mx(
+                        out=acc[:],
+                        lhsT=s_codes[:, g * B : (g + 1) * B].bitcast(FP8X4),
+                        lhsT_scale=s_scales[:, g * B : (g + 1) * B],
+                        rhs=w_codes[e][:, k * H1 : (k + 1) * H1].bitcast(FP8X4),
+                        rhs_scale=w_scales[e][:, k * H1 : (k + 1) * H1],
+                        start=(k == 0),
+                        stop=(k == PASSES - 1),
+                    )
+            finish_expert(e, acc)

@@ -21,7 +21,7 @@ PASSES = D // K_PASS
 CHUNK = 1024
 CHUNKS = D // CHUNK
 CHUNK_PASSES = CHUNK // K_PASS
-PAIRS = N // 2
+TERMS = N - 1
 W_HALF_PASSES = PASSES // 2
 W_PIECE_PASSES = 4
 W_PIECES = PASSES // W_PIECE_PASSES
@@ -39,7 +39,7 @@ def tile_softmoedynamics_pa_k_kernel(tc, tokens, logits, W1, b1, g1, be1, out):
         w_raw_pool = ctx.enter_context(tc.tile_pool(name="w_raw", bufs=2))
         w_grp_pool = ctx.enter_context(tc.tile_pool(name="w_grp", bufs=2))
         w_mx_pool = ctx.enter_context(tc.tile_pool(name="w_mx", bufs=2))
-        term_pool = ctx.enter_context(tc.tile_pool(name="term", bufs=6))
+        term_pool = ctx.enter_context(tc.tile_pool(name="term", bufs=8))
         slot_pool = ctx.enter_context(tc.tile_pool(name="slot", bufs=2))
         epi_pool = ctx.enter_context(tc.tile_pool(name="epi", bufs=2))
         turned_pool = ctx.enter_context(tc.psum_pool(name="turned", bufs=6))
@@ -52,10 +52,10 @@ def tile_softmoedynamics_pa_k_kernel(tc, tokens, logits, W1, b1, g1, be1, out):
 
         def load_tokens(c):
             tok_c = tok_pool.tile([P, N, CHUNK], BF16, name="tok%d" % c)
-            for q in range(PAIRS):
+            for n in range(0, N, 2):
                 nc.sync.dma_start(
-                    out=tok_c[:, 2 * q : 2 * q + 2, :],
-                    in_=tokens[:, 2 * q : 2 * q + 2, c * CHUNK : (c + 1) * CHUNK],
+                    out=tok_c[:, n : n + 2, :],
+                    in_=tokens[:, n : n + 2, c * CHUNK : (c + 1) * CHUNK],
                 )
             tok.append(tok_c)
 
@@ -181,24 +181,28 @@ def tile_softmoedynamics_pa_k_kernel(tc, tokens, logits, W1, b1, g1, be1, out):
                 turned = [
                     turned_pool.tile([P, PACK, B], F32, name="turned") for g in range(CHUNK_PASSES)
                 ]
-                for q in range(PAIRS):
+                for n in range(TERMS):
                     term = term_pool.tile([P, CHUNK], F32, name="term")
-                    nc.scalar.activation(
-                        out=term[:], in_=tok[c][:, 2 * q, :], func=ACT.Copy,
-                        scale=disp[:, e, 2 * q : 2 * q + 1],
-                    )
-                    nc.vector.scalar_tensor_tensor(
-                        out=term[:], in0=tok[c][:, 2 * q + 1, :],
-                        scalar=disp[:, e, 2 * q + 1 : 2 * q + 2], in1=term[:],
-                        op0=ALU.mult, op1=ALU.add,
-                    )
+                    if n % 3 == 0:
+                        nc.scalar.activation(
+                            out=term[:], in_=tok[c][:, n, :], func=ACT.Copy, scale=disp[:, e, n : n + 1]
+                        )
+                    else:
+                        nc.vector.tensor_scalar_mul(
+                            out=term[:], in0=tok[c][:, n, :], scalar1=disp[:, e, n : n + 1]
+                        )
+                    if n == 0:
+                        nc.vector.scalar_tensor_tensor(
+                            out=term[:], in0=tok[c][:, N - 1, :], scalar=disp[:, e, N - 1 : N],
+                            in1=term[:], op0=ALU.mult, op1=ALU.add,
+                        )
                     for g in range(CHUNK_PASSES):
                         for t in range(PACK):
                             first = (g * PACK + t) * P
                             nc.tensor.matmul(
                                 out=turned[g][:, t, :], lhsT=term[:, first : first + P], rhs=ident[:],
                                 is_transpose=True,
-                                start=(q == 0 and t == 0), stop=(q == PAIRS - 1 and t == PACK - 1),
+                                start=(n == 0 and t == 0), stop=(n == TERMS - 1 and t == PACK - 1),
                             )
 
                 grouped = slot_pool.tile([P, CHUNK_PASSES, B, PACK], BF16, name="grouped", align_bytes=64)

@@ -17,15 +17,14 @@ EPS = 1e-5
 P = 128
 PACK = 4
 K_PASS = P * PACK
-PASSES = D // K_PASS
 CHUNK = 1024
 CHUNKS = D // CHUNK
 CHUNK_PASSES = CHUNK // K_PASS
-TERMS = N - 1
-W_HALF_PASSES = PASSES // 2
-W_PIECE_PASSES = 4
-W_PIECES = PASSES // W_PIECE_PASSES
-W_PIECE_COLS = W_PIECE_PASSES * H1
+UNITS = E * CHUNKS
+W_UNITS = 2
+W_PASSES = W_UNITS * CHUNK_PASSES
+W_PIECES = UNITS // W_UNITS
+PAIRS = N // 2
 MISH_CLAMP = 20.0
 
 FLOPS = 2 * E * B * D * H1 + 2 * B * N * E * D
@@ -36,47 +35,64 @@ def tile_softmoedynamics_pa_k_kernel(tc, tokens, logits, W1, b1, g1, be1, out):
     with ExitStack() as ctx:
         const = ctx.enter_context(tc.tile_pool(name="const", bufs=1))
         tok_pool = ctx.enter_context(tc.tile_pool(name="tok", bufs=1))
-        w_raw_pool = ctx.enter_context(tc.tile_pool(name="w_raw", bufs=2))
+        w_raw_pool = ctx.enter_context(tc.tile_pool(name="w_raw", bufs=3))
         w_grp_pool = ctx.enter_context(tc.tile_pool(name="w_grp", bufs=2))
-        w_mx_pool = ctx.enter_context(tc.tile_pool(name="w_mx", bufs=2))
+        w_mx_pool = ctx.enter_context(tc.tile_pool(name="w_mx", bufs=3))
         term_pool = ctx.enter_context(tc.tile_pool(name="term", bufs=8))
-        slot_pool = ctx.enter_context(tc.tile_pool(name="slot", bufs=2))
+        slot_pool = ctx.enter_context(tc.tile_pool(name="slot", bufs=3))
         epi_pool = ctx.enter_context(tc.tile_pool(name="epi", bufs=2))
-        turned_pool = ctx.enter_context(tc.psum_pool(name="turned", bufs=6))
-        acc_pool = ctx.enter_context(tc.psum_pool(name="acc", bufs=2))
+        mish_pool = ctx.enter_context(tc.tile_pool(name="mish", bufs=1))
+        turned_pool = ctx.enter_context(tc.psum_pool(name="turned", bufs=7))
+        acc_pool = ctx.enter_context(tc.psum_pool(name="acc", bufs=1))
 
-        lg = const.tile([P, N, E], BF16)
-        nc.sync.dma_start(out=lg[:], in_=logits)
+        tok = [tok_pool.tile([P, N, CHUNK], BF16, name="tok%d" % c) for c in range(CHUNKS)]
 
-        tok = []
-
-        def load_tokens(c):
-            tok_c = tok_pool.tile([P, N, CHUNK], BF16, name="tok%d" % c)
-            for n in range(0, N, 2):
-                nc.sync.dma_start(
-                    out=tok_c[:, n : n + 2, :],
-                    in_=tokens[:, n : n + 2, c * CHUNK : (c + 1) * CHUNK],
-                )
-            tok.append(tok_c)
+        def load_tokens(c, q):
+            agents = slice(2 * q, 2 * q + 2)
+            nc.sync.dma_start(
+                out=tok[c][:, agents, :], in_=tokens[:, agents, c * CHUNK : (c + 1) * CHUNK]
+            )
 
         w_raw = {}
+        w_codes = {}
+        w_scales = {}
 
-        def load_w_half(e, half):
-            raw = w_raw_pool.tile([P, PACK, W_HALF_PASSES * H1], BF16, name="w_raw")
-            rows = W1[e, half * W_HALF_PASSES * K_PASS : (half + 1) * W_HALF_PASSES * K_PASS, :]
+        def load_w(piece):
+            first = piece * W_PASSES * K_PASS
+            raw = w_raw_pool.tile([P, PACK, W_PASSES * H1], BF16, name="w_raw")
+            rows = W1.rearrange("e d h -> (e d) h")[first : first + W_PASSES * K_PASS, :]
             by_code = rows.rearrange("(g t p) h -> t p g h", t=PACK, p=P)
             for t in range(PACK):
                 nc.sync.dma_start(
                     out=raw[:, t, :].rearrange("p (g h) -> p g h", h=H1), in_=by_code[t]
                 )
-            w_raw[(e, half)] = raw
+            w_raw[piece] = raw
 
-        load_tokens(0)
-        load_w_half(0, 0)
-        load_tokens(1)
-        load_w_half(0, 1)
+        def quantise_w(piece):
+            grouped = w_grp_pool.tile([P, W_PASSES * H1, PACK], BF16, name="w_grp", align_bytes=64)
+            nc.vector.tensor_copy(
+                out=grouped[:].rearrange("p (c i) t -> p c t i", i=4),
+                in_=w_raw[piece][:].rearrange("p t (c i) -> p c t i", i=4),
+            )
+            w_codes[piece] = w_mx_pool.tile([P, W_PASSES * H1], U32, name="w_codes", align_bytes=64)
+            w_scales[piece] = w_mx_pool.tile([P, W_PASSES * H1], U8, name="w_scales", align_bytes=64)
+            nc.vector.quantize_mx(
+                out=w_codes[piece][:].bitcast(FP8X4),
+                scales=w_scales[piece][:],
+                in_=grouped[:].rearrange("p w t -> p (w t)"),
+            )
+
+        lg = const.tile([P, N, E], BF16)
+        nc.sync.dma_start(out=lg[:], in_=logits)
+        for q in range(PAIRS):
+            load_tokens(0, q)
+        load_w(0)
+        for q in range(PAIRS):
+            load_tokens(1, q)
+        load_w(1)
         for c in range(2, CHUNKS):
-            load_tokens(c)
+            for q in range(PAIRS):
+                load_tokens(c, q)
 
         bias_bc = const.tile([P, E * H1], BF16)
         gain_bc = const.tile([P, E * H1], BF16)
@@ -90,6 +106,8 @@ def tile_softmoedynamics_pa_k_kernel(tc, tokens, logits, W1, b1, g1, be1, out):
         make_identity(nc, ident[:])
         minus_half = const.tile([P, 1], F32)
         nc.vector.memset(minus_half[:], -0.5)
+        warm = const.tile([P, 1], F32)
+        nc.scalar.activation(out=warm[:], in_=minus_half[:], func=ACT.Exp)
 
         lg_en = lg[:].rearrange("p n e -> p e n")
         top = const.tile([P, E], F32)
@@ -106,41 +124,15 @@ def tile_softmoedynamics_pa_k_kernel(tc, tokens, logits, W1, b1, g1, be1, out):
             out=disp[:], in0=disp[:], in1=total[:].unsqueeze(2).to_broadcast([P, E, N]), op=ALU.mult
         )
 
-        w_codes = {}
-        w_scales = {}
+        quantise_w(0)
 
-        def new_w_mx(e):
-            w_codes[e] = w_mx_pool.tile([P, PASSES * H1], U32, name="w_codes", align_bytes=64)
-            w_scales[e] = w_mx_pool.tile([P, PASSES * H1], U8, name="w_scales", align_bytes=64)
+        v = const.tile([P, E * H1], F32)
 
-        def quantise_w_piece(e, piece):
-            pieces_per_half = W_PIECES // 2
-            raw = w_raw[(e, piece // pieces_per_half)]
-            first = (piece % pieces_per_half) * W_PIECE_COLS
-            grouped = w_grp_pool.tile([P, W_PIECE_COLS, PACK], BF16, name="w_grp", align_bytes=64)
-            nc.vector.tensor_copy(
-                out=grouped[:].rearrange("p (c i) t -> p c t i", i=4),
-                in_=raw[:, :, first : first + W_PIECE_COLS].rearrange("p t (c i) -> p c t i", i=4),
-            )
-            cols = slice(piece * W_PIECE_COLS, (piece + 1) * W_PIECE_COLS)
-            nc.vector.quantize_mx(
-                out=w_codes[e][:, cols].bitcast(FP8X4),
-                scales=w_scales[e][:, cols],
-                in_=grouped[:].rearrange("p w t -> p (w t)"),
-            )
-
-        new_w_mx(0)
-        for piece in range(W_PIECES):
-            quantise_w_piece(0, piece)
-        load_w_half(1, 0)
-        load_w_half(1, 1)
-
-        def finish_expert(e, acc):
+        def layer_norm(e, acc):
             cols = slice(e * H1, (e + 1) * H1)
-            v = epi_pool.tile([P, H1], F32, name="v")
-            nc.vector.tensor_tensor(out=v[:], in0=acc[:], in1=bias_bc[:, cols], op=ALU.add)
+            nc.vector.tensor_tensor(out=v[:, cols], in0=acc[:], in1=bias_bc[:, cols], op=ALU.add)
             stats = epi_pool.tile([P, 6], F32, name="stats")
-            nc.vector.bn_stats(out=stats[:], in_=v[:])
+            nc.vector.bn_stats(out=stats[:], in_=v[:, cols])
             mean_var = epi_pool.tile([P, 2], F32, name="mean_var")
             nc.vector.bn_aggr(out=mean_var[:], in_=stats[:])
             rstd = epi_pool.tile([P, 1], F32, name="rstd")
@@ -148,82 +140,99 @@ def tile_softmoedynamics_pa_k_kernel(tc, tokens, logits, W1, b1, g1, be1, out):
                 out=rstd[:], in0=mean_var[:, 1:2], scalar1=EPS, scalar2=1.0, op0=ALU.add, op1=ALU.mult
             )
             nc.gpsimd.tensor_tensor(out=rstd[:], in0=rstd[:], in1=minus_half[:], op=ALU.pow)
-            nc.vector.tensor_scalar(
-                out=v[:], in0=v[:], scalar1=mean_var[:, 0:1], scalar2=rstd[:],
+            nc.vector.scalar_tensor_tensor(
+                out=v[:, cols], in0=v[:, cols], scalar=mean_var[:, 0:1], in1=gain_bc[:, cols],
                 op0=ALU.subtract, op1=ALU.mult,
             )
-            nc.vector.tensor_tensor(out=v[:], in0=v[:], in1=gain_bc[:, cols], op=ALU.mult)
-            nc.vector.tensor_tensor(out=v[:], in0=v[:], in1=shift_bc[:, cols], op=ALU.add)
-            w = epi_pool.tile([P, H1], F32, name="w")
-            nc.vector.tensor_scalar_min(out=w[:], in0=v[:], scalar1=MISH_CLAMP)
-            nc.scalar.activation(out=w[:], in_=w[:], func=ACT.Exp)
-            n = epi_pool.tile([P, H1], F32, name="n")
             nc.vector.scalar_tensor_tensor(
-                out=n[:], in0=w[:], scalar=2.0, in1=w[:], op0=ALU.add, op1=ALU.mult
+                out=v[:, cols], in0=v[:, cols], scalar=rstd[:], in1=shift_bc[:, cols],
+                op0=ALU.mult, op1=ALU.add,
             )
-            nc.vector.tensor_scalar_add(out=w[:], in0=n[:], scalar1=2.0)
-            nc.vector.reciprocal(out=w[:], in_=w[:])
-            nc.vector.tensor_tensor(out=n[:], in0=n[:], in1=v[:], op=ALU.mult)
-            nc.vector.tensor_tensor(out=n[:], in0=n[:], in1=w[:], op=ALU.mult)
-            nc.sync.dma_start(out=out[:, e, :], in_=n[:])
 
-        for e in range(E):
-            acc = acc_pool.tile([P, H1], F32, name="acc")
-            if e + 1 < E:
-                new_w_mx(e + 1)
-            for c in range(CHUNKS):
-                if e + 1 < E and c % 2 == 0:
-                    piece = c // 2
-                    quantise_w_piece(e + 1, piece)
-                    if e + 2 < E and piece % 2 == 1:
-                        load_w_half(e + 2, piece // 2)
+        w = mish_pool.tile([P, E * H1], F32)
+        numer = mish_pool.tile([P, E * H1], F32)
 
-                turned = [
-                    turned_pool.tile([P, PACK, B], F32, name="turned") for g in range(CHUNK_PASSES)
-                ]
-                for n in range(TERMS):
-                    term = term_pool.tile([P, CHUNK], F32, name="term")
-                    if n % 3 == 0:
-                        nc.scalar.activation(
-                            out=term[:], in_=tok[c][:, n, :], func=ACT.Copy, scale=disp[:, e, n : n + 1]
-                        )
-                    else:
-                        nc.vector.tensor_scalar_mul(
-                            out=term[:], in0=tok[c][:, n, :], scalar1=disp[:, e, n : n + 1]
-                        )
-                    if n == 0:
-                        nc.vector.scalar_tensor_tensor(
-                            out=term[:], in0=tok[c][:, N - 1, :], scalar=disp[:, e, N - 1 : N],
-                            in1=term[:], op0=ALU.mult, op1=ALU.add,
-                        )
-                    for g in range(CHUNK_PASSES):
-                        for t in range(PACK):
-                            first = (g * PACK + t) * P
-                            nc.tensor.matmul(
-                                out=turned[g][:, t, :], lhsT=term[:, first : first + P], rhs=ident[:],
-                                is_transpose=True,
-                                start=(n == 0 and t == 0), stop=(n == TERMS - 1 and t == PACK - 1),
-                            )
+        def mish_and_store(first_e, last_e):
+            cols = slice(first_e * H1, last_e * H1)
+            nc.vector.tensor_scalar_min(out=w[:, cols], in0=v[:, cols], scalar1=MISH_CLAMP)
+            nc.scalar.activation(out=w[:, cols], in_=w[:, cols], func=ACT.Exp)
+            nc.vector.scalar_tensor_tensor(
+                out=numer[:, cols], in0=w[:, cols], scalar=2.0, in1=w[:, cols], op0=ALU.add, op1=ALU.mult
+            )
+            nc.vector.tensor_scalar_add(out=w[:, cols], in0=numer[:, cols], scalar1=2.0)
+            nc.vector.reciprocal(out=w[:, cols], in_=w[:, cols])
+            nc.vector.tensor_tensor(out=numer[:, cols], in0=numer[:, cols], in1=v[:, cols], op=ALU.mult)
+            nc.vector.tensor_tensor(out=numer[:, cols], in0=numer[:, cols], in1=w[:, cols], op=ALU.mult)
+            nc.sync.dma_start(
+                out=out[:, first_e:last_e, :].rearrange("b e h -> b (e h)"), in_=numer[:, cols]
+            )
 
-                grouped = slot_pool.tile([P, CHUNK_PASSES, B, PACK], BF16, name="grouped", align_bytes=64)
+        for u in range(UNITS):
+            e, c = divmod(u, CHUNKS)
+            piece = u // W_UNITS
+            if u % W_UNITS == 0 and piece + 2 < W_PIECES:
+                load_w(piece + 2)
+            if u % W_UNITS == 0 and piece + 1 < W_PIECES:
+                quantise_w(piece + 1)
+            if c == 0:
+                acc = acc_pool.tile([P, H1], F32, name="acc")
+
+            turned = [turned_pool.tile([P, PACK, B], F32, name="turned") for g in range(CHUNK_PASSES)]
+
+            def add_turned(term, opens, closes):
                 for g in range(CHUNK_PASSES):
-                    nc.scalar.copy(out=grouped[:, g, :, :], in_=turned[g][:].rearrange("p t b -> p b t"))
-                s_codes = slot_pool.tile([P, CHUNK_PASSES * B], U32, name="s_codes", align_bytes=64)
-                s_scales = slot_pool.tile([P, CHUNK_PASSES * B], U8, name="s_scales", align_bytes=64)
-                nc.vector.quantize_mx(
-                    out=s_codes[:].bitcast(FP8X4),
-                    scales=s_scales[:],
-                    in_=grouped[:].rearrange("p g b t -> p (g b t)"),
+                    for t in range(PACK):
+                        first = (g * PACK + t) * P
+                        nc.tensor.matmul(
+                            out=turned[g][:, t, :], lhsT=term[:, first : first + P], rhs=ident[:],
+                            is_transpose=True,
+                            start=(opens and t == 0), stop=(closes and t == PACK - 1),
+                        )
+
+            for q in range(PAIRS):
+                even, odd = 2 * q, 2 * q + 1
+                split = q == PAIRS - 1 and c % 2 == 1
+                term = term_pool.tile([P, CHUNK], F32, name="term")
+                nc.scalar.activation(
+                    out=term[:], in_=tok[c][:, even, :], func=ACT.Copy, scale=disp[:, e, even : even + 1]
                 )
-                for g in range(CHUNK_PASSES):
-                    k = c * CHUNK_PASSES + g
-                    nc.tensor.matmul_mx(
-                        out=acc[:],
-                        lhsT=s_codes[:, g * B : (g + 1) * B].bitcast(FP8X4),
-                        lhsT_scale=s_scales[:, g * B : (g + 1) * B],
-                        rhs=w_codes[e][:, k * H1 : (k + 1) * H1].bitcast(FP8X4),
-                        rhs_scale=w_scales[e][:, k * H1 : (k + 1) * H1],
-                        start=(k == 0),
-                        stop=(k == PASSES - 1),
+                if split:
+                    add_turned(term, False, False)
+                    term = term_pool.tile([P, CHUNK], F32, name="term")
+                    nc.vector.tensor_scalar_mul(
+                        out=term[:], in0=tok[c][:, odd, :], scalar1=disp[:, e, odd : odd + 1]
                     )
-            finish_expert(e, acc)
+                else:
+                    nc.vector.scalar_tensor_tensor(
+                        out=term[:], in0=tok[c][:, odd, :], scalar=disp[:, e, odd : odd + 1], in1=term[:],
+                        op0=ALU.mult, op1=ALU.add,
+                    )
+                add_turned(term, q == 0, q == PAIRS - 1)
+
+            if u == UNITS - 1:
+                mish_and_store(0, E - 1)
+
+            grouped = slot_pool.tile([P, CHUNK_PASSES, B, PACK], BF16, name="grouped", align_bytes=64)
+            for g in range(CHUNK_PASSES):
+                nc.scalar.copy(out=grouped[:, g, :, :], in_=turned[g][:].rearrange("p t b -> p b t"))
+            s_codes = slot_pool.tile([P, CHUNK_PASSES * B], U32, name="s_codes", align_bytes=64)
+            s_scales = slot_pool.tile([P, CHUNK_PASSES * B], U8, name="s_scales", align_bytes=64)
+            nc.vector.quantize_mx(
+                out=s_codes[:].bitcast(FP8X4),
+                scales=s_scales[:],
+                in_=grouped[:].rearrange("p g b t -> p (g b t)"),
+            )
+            for g in range(CHUNK_PASSES):
+                w_cols = slice(((u % W_UNITS) * CHUNK_PASSES + g) * H1, ((u % W_UNITS) * CHUNK_PASSES + g + 1) * H1)
+                nc.tensor.matmul_mx(
+                    out=acc[:],
+                    lhsT=s_codes[:, g * B : (g + 1) * B].bitcast(FP8X4),
+                    lhsT_scale=s_scales[:, g * B : (g + 1) * B],
+                    rhs=w_codes[piece][:, w_cols].bitcast(FP8X4),
+                    rhs_scale=w_scales[piece][:, w_cols],
+                    start=(c == 0 and g == 0),
+                    stop=(c == CHUNKS - 1 and g == CHUNK_PASSES - 1),
+                )
+            if c == CHUNKS - 1:
+                layer_norm(e, acc)
+        mish_and_store(E - 1, E)

from contextlib import ExitStack

import concourse.mybir as mybir
from concourse.masks import make_identity

F32 = mybir.dt.float32
BF16 = mybir.dt.bfloat16
U32 = mybir.dt.uint32
U8 = mybir.dt.uint8
FP8X4 = mybir.dt.float8_e4m3fn_x4
ALU = mybir.AluOpType
ACT = mybir.ActivationFunctionType
AXIS = mybir.AxisListType

B, N, E, D, H1 = 128, 8, 8, 8192, 128
EPS = 1e-5
P = 128
PACK = 4
K_PASS = P * PACK
CHUNK = 1024
CHUNKS = D // CHUNK
CHUNK_PASSES = CHUNK // K_PASS
UNITS = E * CHUNKS
W_UNITS = 2
W_PASSES = W_UNITS * CHUNK_PASSES
W_PIECES = UNITS // W_UNITS
PAIRS = N // 2
MISH_CLAMP = 20.0

FLOPS = 2 * E * B * D * H1 + 2 * B * N * E * D


def tile_softmoedynamics_pa_k_kernel(tc, tokens, logits, W1, b1, g1, be1, out):
    nc = tc.nc
    with ExitStack() as ctx:
        const = ctx.enter_context(tc.tile_pool(name="const", bufs=1))
        tok_pool = ctx.enter_context(tc.tile_pool(name="tok", bufs=1))
        w_raw_pool = ctx.enter_context(tc.tile_pool(name="w_raw", bufs=3))
        w_grp_pool = ctx.enter_context(tc.tile_pool(name="w_grp", bufs=2))
        w_mx_pool = ctx.enter_context(tc.tile_pool(name="w_mx", bufs=3))
        term_pool = ctx.enter_context(tc.tile_pool(name="term", bufs=8))
        slot_pool = ctx.enter_context(tc.tile_pool(name="slot", bufs=3))
        epi_pool = ctx.enter_context(tc.tile_pool(name="epi", bufs=2))
        mish_pool = ctx.enter_context(tc.tile_pool(name="mish", bufs=1))
        turned_pool = ctx.enter_context(tc.psum_pool(name="turned", bufs=7))
        acc_pool = ctx.enter_context(tc.psum_pool(name="acc", bufs=1))

        tok = [tok_pool.tile([P, N, CHUNK], BF16, name="tok%d" % c) for c in range(CHUNKS)]

        def load_tokens(c, q):
            agents = slice(2 * q, 2 * q + 2)
            nc.sync.dma_start(
                out=tok[c][:, agents, :], in_=tokens[:, agents, c * CHUNK : (c + 1) * CHUNK]
            )

        w_raw = {}
        w_codes = {}
        w_scales = {}

        def load_w(piece):
            first = piece * W_PASSES * K_PASS
            raw = w_raw_pool.tile([P, PACK, W_PASSES * H1], BF16, name="w_raw")
            rows = W1.rearrange("e d h -> (e d) h")[first : first + W_PASSES * K_PASS, :]
            by_code = rows.rearrange("(g t p) h -> t p g h", t=PACK, p=P)
            for t in range(PACK):
                nc.sync.dma_start(
                    out=raw[:, t, :].rearrange("p (g h) -> p g h", h=H1), in_=by_code[t]
                )
            w_raw[piece] = raw

        def quantise_w(piece):
            grouped = w_grp_pool.tile([P, W_PASSES * H1, PACK], BF16, name="w_grp", align_bytes=64)
            nc.vector.tensor_copy(
                out=grouped[:].rearrange("p (c i) t -> p c t i", i=4),
                in_=w_raw[piece][:].rearrange("p t (c i) -> p c t i", i=4),
            )
            w_codes[piece] = w_mx_pool.tile([P, W_PASSES * H1], U32, name="w_codes", align_bytes=64)
            w_scales[piece] = w_mx_pool.tile([P, W_PASSES * H1], U8, name="w_scales", align_bytes=64)
            nc.vector.quantize_mx(
                out=w_codes[piece][:].bitcast(FP8X4),
                scales=w_scales[piece][:],
                in_=grouped[:].rearrange("p w t -> p (w t)"),
            )

        lg = const.tile([P, N, E], BF16)
        nc.sync.dma_start(out=lg[:], in_=logits)
        for q in range(PAIRS):
            load_tokens(0, q)
        load_w(0)
        for q in range(PAIRS):
            load_tokens(1, q)
        load_w(1)
        for c in range(2, CHUNKS):
            for q in range(PAIRS):
                load_tokens(c, q)

        bias_bc = const.tile([P, E * H1], BF16)
        gain_bc = const.tile([P, E * H1], BF16)
        shift_bc = const.tile([P, E * H1], BF16)
        for row_bc, vec in ((bias_bc, b1), (gain_bc, g1), (shift_bc, be1)):
            nc.gpsimd.dma_start(
                out=row_bc[:], in_=vec.rearrange("e h -> (e h)").partition_broadcast(P)
            )

        ident = const.tile([P, P], F32)
        make_identity(nc, ident[:])
        minus_half = const.tile([P, 1], F32)
        nc.vector.memset(minus_half[:], -0.5)
        warm = const.tile([P, 1], F32)
        nc.scalar.activation(out=warm[:], in_=minus_half[:], func=ACT.Exp)

        lg_en = lg[:].rearrange("p n e -> p e n")
        top = const.tile([P, E], F32)
        nc.vector.tensor_reduce(out=top[:], in_=lg_en, axis=AXIS.X, op=ALU.max)
        disp = const.tile([P, E, N], F32)
        nc.vector.tensor_tensor(
            out=disp[:], in0=lg_en, in1=top[:].unsqueeze(2).to_broadcast([P, E, N]), op=ALU.subtract
        )
        nc.scalar.activation(out=disp[:], in_=disp[:], func=ACT.Exp)
        total = const.tile([P, E], F32)
        nc.vector.tensor_reduce(out=total[:], in_=disp[:], axis=AXIS.X, op=ALU.add)
        nc.vector.reciprocal(out=total[:], in_=total[:])
        nc.vector.tensor_tensor(
            out=disp[:], in0=disp[:], in1=total[:].unsqueeze(2).to_broadcast([P, E, N]), op=ALU.mult
        )

        quantise_w(0)

        v = const.tile([P, E * H1], F32)

        def layer_norm(e, acc):
            cols = slice(e * H1, (e + 1) * H1)
            nc.vector.tensor_tensor(out=v[:, cols], in0=acc[:], in1=bias_bc[:, cols], op=ALU.add)
            stats = epi_pool.tile([P, 6], F32, name="stats")
            nc.vector.bn_stats(out=stats[:], in_=v[:, cols])
            mean_var = epi_pool.tile([P, 2], F32, name="mean_var")
            nc.vector.bn_aggr(out=mean_var[:], in_=stats[:])
            rstd = epi_pool.tile([P, 1], F32, name="rstd")
            nc.gpsimd.tensor_scalar(
                out=rstd[:], in0=mean_var[:, 1:2], scalar1=EPS, scalar2=1.0, op0=ALU.add, op1=ALU.mult
            )
            nc.gpsimd.tensor_tensor(out=rstd[:], in0=rstd[:], in1=minus_half[:], op=ALU.pow)
            nc.vector.scalar_tensor_tensor(
                out=v[:, cols], in0=v[:, cols], scalar=mean_var[:, 0:1], in1=gain_bc[:, cols],
                op0=ALU.subtract, op1=ALU.mult,
            )
            nc.vector.scalar_tensor_tensor(
                out=v[:, cols], in0=v[:, cols], scalar=rstd[:], in1=shift_bc[:, cols],
                op0=ALU.mult, op1=ALU.add,
            )

        w = mish_pool.tile([P, E * H1], F32)
        numer = mish_pool.tile([P, E * H1], F32)

        def mish_and_store(first_e, last_e):
            cols = slice(first_e * H1, last_e * H1)
            nc.vector.tensor_scalar_min(out=w[:, cols], in0=v[:, cols], scalar1=MISH_CLAMP)
            nc.scalar.activation(out=w[:, cols], in_=w[:, cols], func=ACT.Exp)
            nc.vector.scalar_tensor_tensor(
                out=numer[:, cols], in0=w[:, cols], scalar=2.0, in1=w[:, cols], op0=ALU.add, op1=ALU.mult
            )
            nc.vector.tensor_scalar_add(out=w[:, cols], in0=numer[:, cols], scalar1=2.0)
            nc.vector.reciprocal(out=w[:, cols], in_=w[:, cols])
            nc.vector.tensor_tensor(out=numer[:, cols], in0=numer[:, cols], in1=v[:, cols], op=ALU.mult)
            nc.vector.tensor_tensor(out=numer[:, cols], in0=numer[:, cols], in1=w[:, cols], op=ALU.mult)
            nc.sync.dma_start(
                out=out[:, first_e:last_e, :].rearrange("b e h -> b (e h)"), in_=numer[:, cols]
            )

        for u in range(UNITS):
            e, c = divmod(u, CHUNKS)
            piece = u // W_UNITS
            if u % W_UNITS == 0 and piece + 2 < W_PIECES:
                load_w(piece + 2)
            if u % W_UNITS == 0 and piece + 1 < W_PIECES:
                quantise_w(piece + 1)
            if c == 0:
                acc = acc_pool.tile([P, H1], F32, name="acc")

            turned = [turned_pool.tile([P, PACK, B], F32, name="turned") for g in range(CHUNK_PASSES)]

            def add_turned(term, opens, closes):
                for g in range(CHUNK_PASSES):
                    for t in range(PACK):
                        first = (g * PACK + t) * P
                        nc.tensor.matmul(
                            out=turned[g][:, t, :], lhsT=term[:, first : first + P], rhs=ident[:],
                            is_transpose=True,
                            start=(opens and t == 0), stop=(closes and t == PACK - 1),
                        )

            for q in range(PAIRS):
                even, odd = 2 * q, 2 * q + 1
                split = q == PAIRS - 1 and c % 2 == 1
                term = term_pool.tile([P, CHUNK], F32, name="term")
                nc.scalar.activation(
                    out=term[:], in_=tok[c][:, even, :], func=ACT.Copy, scale=disp[:, e, even : even + 1]
                )
                if split:
                    add_turned(term, False, False)
                    term = term_pool.tile([P, CHUNK], F32, name="term")
                    nc.vector.tensor_scalar_mul(
                        out=term[:], in0=tok[c][:, odd, :], scalar1=disp[:, e, odd : odd + 1]
                    )
                else:
                    nc.vector.scalar_tensor_tensor(
                        out=term[:], in0=tok[c][:, odd, :], scalar=disp[:, e, odd : odd + 1], in1=term[:],
                        op0=ALU.mult, op1=ALU.add,
                    )
                add_turned(term, q == 0, q == PAIRS - 1)

            if u == UNITS - 1:
                mish_and_store(0, E - 1)

            grouped = slot_pool.tile([P, CHUNK_PASSES, B, PACK], BF16, name="grouped", align_bytes=64)
            for g in range(CHUNK_PASSES):
                nc.scalar.copy(out=grouped[:, g, :, :], in_=turned[g][:].rearrange("p t b -> p b t"))
            s_codes = slot_pool.tile([P, CHUNK_PASSES * B], U32, name="s_codes", align_bytes=64)
            s_scales = slot_pool.tile([P, CHUNK_PASSES * B], U8, name="s_scales", align_bytes=64)
            nc.vector.quantize_mx(
                out=s_codes[:].bitcast(FP8X4),
                scales=s_scales[:],
                in_=grouped[:].rearrange("p g b t -> p (g b t)"),
            )
            for g in range(CHUNK_PASSES):
                w_cols = slice(((u % W_UNITS) * CHUNK_PASSES + g) * H1, ((u % W_UNITS) * CHUNK_PASSES + g + 1) * H1)
                nc.tensor.matmul_mx(
                    out=acc[:],
                    lhsT=s_codes[:, g * B : (g + 1) * B].bitcast(FP8X4),
                    lhsT_scale=s_scales[:, g * B : (g + 1) * B],
                    rhs=w_codes[piece][:, w_cols].bitcast(FP8X4),
                    rhs_scale=w_scales[piece][:, w_cols],
                    start=(c == 0 and g == 0),
                    stop=(c == CHUNKS - 1 and g == CHUNK_PASSES - 1),
                )
            if c == CHUNKS - 1:
                layer_norm(e, acc)
        mish_and_store(E - 1, E)
